import numpy as np
import ml_dtypes


def mxq(x, axis, fmt="e4m3"):
    dtype, down = {"e4m3": (ml_dtypes.float8_e4m3fn, 7), "e5m2": (ml_dtypes.float8_e5m2, 14)}[fmt]
    v = np.moveaxis(np.asarray(x, np.float32).astype(ml_dtypes.bfloat16).astype(np.float64), axis, -1)
    blocks = v.reshape(v.shape[:-1] + (-1, 32))
    amax = np.abs(blocks).max(-1, keepdims=True)
    byte = np.maximum(np.where(amax > 0, np.frexp(amax)[1] - 1 + 127, 0) - down, 1)
    scale = np.exp2(byte - 127.0)
    codes = (blocks / scale).astype(np.float32).astype(dtype).astype(np.float64)
    return np.moveaxis((codes * scale).reshape(v.shape), -1, axis)


WIDE = False


def mx_kscale(k):
    if not WIDE:
        return np.ones(k)
    levels = np.array([10, -10, 5, -5, 0])
    a = np.random.permutation(np.resize(levels, k // 512 * 4)).reshape(k // 512, 4)
    idx = np.arange(k)
    return np.exp2(a[idx // 512, idx % 128 // 32])


BF16 = ml_dtypes.bfloat16


def bf(x):
    return np.asarray(x, np.float32).astype(BF16)


def f64(x):
    return np.asarray(x).astype(np.float64)


B, L, E, H = 4, 64, 2048, 16
HD = E // H
EPS = 1e-12


def l2_normalize(t):
    n = np.sqrt(np.sum(t * t, axis=-1, keepdims=True))
    return t / np.maximum(n, EPS)


def setup_inputs():
    s = mx_kscale(E)
    return {"x": bf(np.random.standard_normal((B, L, E)) * s),
            "W": bf(np.random.standard_normal((3 * E, E)) / np.sqrt(E) / s[None, :]),
            "b": bf(np.random.standard_normal(3 * E) * 0.3)}


def reference(x, W, b):
    y = (mxq(f64(x), 2, "e4m3") @ mxq(f64(W), 1, "e4m3").T) + f64(b)
    y = y.reshape(B, L, H, 3, HD)
    q = np.transpose(y[..., 0, :], (0, 2, 1, 3))
    k = np.transpose(y[..., 1, :], (0, 2, 1, 3))
    v = np.transpose(y[..., 2, :], (0, 2, 1, 3))
    return l2_normalize(q), l2_normalize(k), v

@@ -1,0 +1,296 @@
+from contextlib import ExitStack
+
+import concourse.mybir as mybir
+from concourse.masks import make_identity
+
+F32 = mybir.dt.float32
+BF16 = mybir.dt.bfloat16
+U32 = mybir.dt.uint32
+U8 = mybir.dt.uint8
+I32 = mybir.dt.int32
+FP8X4 = mybir.dt.float8_e4m3fn_x4
+ALU = mybir.AluOpType
+ACT = mybir.ActivationFunctionType
+
+P = 128
+E = 2048
+NH = 16
+HD = 128
+NBLK = 12
+NPAIR = 24
+NW = 6
+FLOPS = 2 * 256 * 2048 * 6144
+
+MANUAL = True
+SCALE_ON_GPSIMD = True
+VECTOR_DRAINS = (3,)
+
+
+def tile_selfattention_pa_kernel(tc, x, W, b, out_0, out_1, out_2):
+    nc = tc.nc
+    outs = (out_0, out_1, out_2)
+    with ExitStack() as ctx:
+        const = ctx.enter_context(tc.tile_pool(name="const", bufs=1))
+        wpool = ctx.enter_context(tc.tile_pool(name="wpool", bufs=NW))
+        gpool = ctx.enter_context(tc.tile_pool(name="gpool", bufs=6))
+        cpool = ctx.enter_context(tc.tile_pool(name="cpool", bufs=6))
+        ypool = ctx.enter_context(tc.tile_pool(name="ypool", bufs=6))
+        spool = ctx.enter_context(tc.tile_pool(name="spool", bufs=4))
+        tpsum = ctx.enter_context(tc.psum_pool(name="tpsum", bufs=5))
+        opsum = ctx.enter_context(tc.psum_pool(name="opsum", bufs=3))
+        if MANUAL:
+            ctx.enter_context(tc.manual_schedule())
+
+        ident_f = const.tile([P, P], F32, name="ident_f")
+        ident_b = const.tile([P, P], BF16, name="ident_b")
+        b_sb = const.tile([P, 384], BF16, name="b_sb")
+        bias_bc = const.tile([P, 6144], BF16, name="bias_bc")
+        warm = const.tile([P, 1], F32, name="warm")
+        warm2 = const.tile([P, 1], F32, name="warm2")
+        x_sb = [const.tile([P, E], BF16, name="x_sb%d" % m) for m in range(2)]
+        xg = const.tile([P, 4096], BF16, name="xg", align_bytes=64)
+        xc = const.tile([P, 1024], U32, name="xc", align_bytes=64)
+        xs = const.tile([P, 1024], U8, name="xs", align_bytes=64)
+
+        w_tiles = {}
+
+        def load_w(i):
+            w_sb = wpool.tile([P, 4 * E], BF16, name="w_sb")
+            nc.sync.dma_start(
+                out=w_sb[:],
+                in_=W[512 * i:512 * (i + 1), :].rearrange("(p t) k -> p (t k)", t=4),
+            )
+            w_tiles[i] = w_sb
+
+        nc.vector.memset(b_sb[:].bitcast(I32), 0)
+        nc.vector.memset(warm[:], 1.0)
+        nc.sync.dma_start(out=b_sb[0:16, :], in_=b.rearrange("(h n) -> h n", h=16))
+        for m in range(2):
+            for bl in range(2):
+                nc.sync.dma_start(out=x_sb[m][bl:P:2, :], in_=x[2 * m + bl, :, :])
+        for i in range(NW):
+            load_w(i)
+        make_identity(nc, ident_b[:])
+        make_identity(nc, ident_f[:])
+        nc.scalar.sqrt(out=warm2[:], in_=warm[:])
+
+        def drain(eng_is_vector, dst, src):
+            if eng_is_vector:
+                nc.vector.tensor_copy(out=dst, in_=src)
+            else:
+                nc.scalar.copy(out=dst, in_=src)
+
+        for h in range(NH):
+            tb = tpsum.tile([P, 512], F32, name="tb")
+            nc.tensor.matmul(
+                out=tb[:, 0:384],
+                lhsT=ident_b[:, h:h + 1].to_broadcast([P, P]),
+                rhs=b_sb[:],
+                start=True,
+                stop=True,
+            )
+            drain(h % 2 == 0, bias_bc[:, 384 * h:384 * (h + 1)], tb[:, 0:384])
+
+        def transposes_into_bank(src32, col0, step_a):
+            tb = tpsum.tile([P, 512], F32, name="tb")
+            for a in range(2):
+                for u in range(2):
+                    c0 = col0 + a * step_a + 128 * u
+                    nc.tensor.transpose(
+                        out=tb[:, (2 * a + u) * P:(2 * a + u + 1) * P],
+                        in_=src32[:, c0:c0 + P],
+                        identity=ident_f[:],
+                    )
+            return tb
+
+        def drain_bank(eng_is_vector, dst32, tb):
+            drain(
+                eng_is_vector,
+                dst32.rearrange("q (a c u) -> q a c u", a=2, u=2),
+                tb[:].rearrange("q (a u c) -> q a c u", a=2, u=2),
+            )
+
+        xg32 = xg[:].bitcast(F32)
+        for m in range(2):
+            x32 = x_sb[m][:].bitcast(F32)
+            for gp in range(2):
+                tb = transposes_into_bank(x32, 512 * gp, 256)
+                w0 = (4 * m + 2 * gp) * 256
+                drain_bank(gp == 0, xg32[:, w0:w0 + 512], tb)
+        nc.vector.quantize_mx(out=xc[:].bitcast(FP8X4), scales=xs[:], in_=xg[:])
+
+        banks = {}
+        grouped = {}
+        codes = {}
+        acc = {}
+        ytile = {}
+        stats = {}
+
+        def stage_t(k):
+            i = k // 2
+            w32 = w_tiles[i][:].bitcast(F32)
+            for un in range(2):
+                g = 2 * (k % 2) + un
+                for tt in range(2):
+                    banks[(k, 2 * un + tt)] = transposes_into_bank(
+                        w32, 2 * tt * 1024 + 256 * g, 1024
+                    )
+
+        def stage_d(k, j):
+            un = j // 2
+            tt = j % 2
+            if tt == 0:
+                grouped[(k, un)] = gpool.tile([P, 2048], BF16, name="grp", align_bytes=64)
+            g32 = grouped[(k, un)][:].bitcast(F32)
+            drain_bank(j in VECTOR_DRAINS, g32[:, 512 * tt:512 * (tt + 1)], banks[(k, j)])
+
+        def stage_q(k, un):
+            cd = cpool.tile([P, 512], U32, name="cd", align_bytes=64)
+            sc = cpool.tile([P, 512], U8, name="sc", align_bytes=64)
+            nc.vector.quantize_mx(
+                out=cd[:].bitcast(FP8X4), scales=sc[:], in_=grouped[(k, un)][:]
+            )
+            codes[(k, un)] = (cd, sc)
+
+        def stage_m(k):
+            i = k // 2
+            for m in range(2):
+                if k % 2 == 0:
+                    acc[(i, m)] = opsum.tile([P, 512], F32, name="acc")
+                for un in range(2):
+                    g = 2 * (k % 2) + un
+                    cd, sc = codes[(k, un)]
+                    xcol = (4 * m + g) * P
+                    nc.tensor.matmul_mx(
+                        out=acc[(i, m)][:],
+                        lhsT=xc[:, xcol:xcol + P].bitcast(FP8X4),
+                        lhsT_scale=xs[:, xcol:xcol + P],
+                        rhs=cd[:].bitcast(FP8X4),
+                        rhs_scale=sc[:],
+                        start=(g == 0),
+                        stop=(g == 3),
+                    )
+
+        def qk_groups(i):
+            return [gq for gq in range(4) if (4 * i + gq) % 3 != 2]
+
+        def stage_a(i, m):
+            if i % 3 == 0:
+                ytile[(i // 3, m)] = ypool.tile([P, 1536], F32, name="y3")
+            off = 512 * (i % 3)
+            nc.vector.tensor_tensor(
+                out=ytile[(i // 3, m)][:, off:off + 512].rearrange("q (p t) -> q p t", t=4),
+                in0=acc[(i, m)][:].rearrange("q (t p) -> q p t", t=4),
+                in1=bias_bc[:, 512 * i:512 * (i + 1)].rearrange("q (p t) -> q p t", t=4),
+                op=ALU.add,
+            )
+
+        def group_ap(i, m, gq):
+            off = 512 * (i % 3) + P * gq
+            return ytile[(i // 3, m)][:, off:off + P]
+
+        def stage_sq(i, m, r):
+            groups = qk_groups(i)
+            n = len(groups)
+            if m == 0 and r == 0:
+                stats[(i, "ss")] = spool.tile([P, 2 * n], F32, name="ss")
+            sq = spool.tile([P, P], F32, name="sq")
+            col = m * n + r
+            nc.scalar.activation(
+                out=sq[:],
+                in_=group_ap(i, m, groups[r]),
+                func=ACT.Square,
+                accum_out=stats[(i, "ss")][:, col:col + 1],
+            )
+
+        def stage_max(i):
+            n = len(qk_groups(i))
+            stats[(i, "sc")] = spool.tile([P, 2 * n], F32, name="ssc")
+            nc.vector.tensor_scalar_max(
+                out=stats[(i, "sc")][:], in0=stats[(i, "ss")][:], scalar1=1e-24
+            )
+
+        def stage_sqrt(i):
+            n = len(qk_groups(i))
+            stats[(i, "nr")] = spool.tile([P, 2 * n], F32, name="nrm")
+            nc.scalar.sqrt(out=stats[(i, "nr")][:], in_=stats[(i, "sc")][:])
+
+        def stage_recip(i):
+            n = len(qk_groups(i))
+            stats[(i, "rn")] = spool.tile([P, 2 * n], F32, name="rn")
+            nc.vector.reciprocal(out=stats[(i, "rn")][:], in_=stats[(i, "nr")][:])
+
+        def stage_scale(i):
+            groups = qk_groups(i)
+            n = len(groups)
+            for m in range(2):
+                for r in range(n):
+                    ap = group_ap(i, m, groups[r])
+                    col = m * n + r
+                    rcol = stats[(i, "rn")][:, col:col + 1]
+                    if SCALE_ON_GPSIMD:
+                        nc.gpsimd.tensor_scalar(
+                            out=ap, in0=ap, scalar1=rcol, scalar2=0.0,
+                            op0=ALU.mult, op1=ALU.add,
+                        )
+                    else:
+                        nc.vector.tensor_scalar_mul(out=ap, in0=ap, scalar1=rcol)
+
+        def stage_store(sb):
+            for m in range(2):
+                for bl in range(2):
+                    view = ytile[(sb, m)][bl:P:2, :].rearrange(
+                        "q (h s c) -> q s h c", s=3, c=HD
+                    )
+                    for s in range(3):
+                        nc.sync.dma_start(
+                            out=outs[s][2 * m + bl, 4 * sb:4 * sb + 4, :, :].rearrange(
+                                "h l c -> l h c"
+                            ),
+                            in_=view[:, s, :, :],
+                        )
+
+        def blk(slot, lag):
+            v = slot - lag
+            if v >= 0 and v % 2 == 0 and v // 2 < NBLK:
+                return v // 2
+            return None
+
+        for k in range(NPAIR + 8):
+            i_rc = blk(k, 7)
+            if i_rc is not None:
+                stage_recip(i_rc)
+                stage_scale(i_rc)
+            i_mx = blk(k, 6)
+            if i_mx is not None:
+                stage_max(i_mx)
+            i_a = blk(k, 4)
+            if i_a is not None:
+                stage_a(i_a, 0)
+                stage_a(i_a, 1)
+            if k < NPAIR:
+                stage_t(k)
+                if k % 2 == 1 and k // 2 + NW < NBLK:
+                    load_w(k // 2 + NW)
+            squares = []
+            if i_a is not None:
+                squares = [(i_a, 0, r) for r in range(len(qk_groups(i_a)))]
+            i_s1 = blk(k, 5)
+            if i_s1 is not None:
+                squares = [(i_s1, 1, r) for r in range(len(qk_groups(i_s1)))]
+            if 1 <= k <= NPAIR:
+                stage_q(k - 1, 0)
+            for j in range(4):
+                if k < NPAIR:
+                    stage_d(k, j)
+                if j < len(squares):
+                    stage_sq(*squares[j])
+            if 1 <= k <= NPAIR:
+                stage_q(k - 1, 1)
+            if i_mx is not None:
+                stage_sqrt(i_mx)
+            if 2 <= k <= NPAIR + 1:
+                stage_m(k - 2)
+            i_st = blk(k, 8)
+            if i_st is not None and i_st % 3 == 2:
+                stage_store(i_st // 3)

@@ -17,13 +17,11 @@ E = 2048
 NH = 16
 HD = 128
 NBLK = 12
-NPAIR = 24
-NW = 6
+NPASS = 4
+W_AHEAD = 5
+T_BANKS = 5
+FLUSH_AFTER = (2, 5, 8, 10, 11)
 FLOPS = 2 * 256 * 2048 * 6144
-
-MANUAL = True
-SCALE_ON_GPSIMD = True
-VECTOR_DRAINS = (3,)
 
 
 def tile_selfattention_pa_kernel(tc, x, W, b, out_0, out_1, out_2):
@@ -31,15 +29,14 @@ def tile_selfattention_pa_kernel(tc, x, W, b, out_0, out_1, out_2):
     outs = (out_0, out_1, out_2)
     with ExitStack() as ctx:
         const = ctx.enter_context(tc.tile_pool(name="const", bufs=1))
-        wpool = ctx.enter_context(tc.tile_pool(name="wpool", bufs=NW))
-        gpool = ctx.enter_context(tc.tile_pool(name="gpool", bufs=6))
-        cpool = ctx.enter_context(tc.tile_pool(name="cpool", bufs=6))
-        ypool = ctx.enter_context(tc.tile_pool(name="ypool", bufs=6))
+        wpool = ctx.enter_context(tc.tile_pool(name="wpool", bufs=2 * W_AHEAD))
+        gpool = ctx.enter_context(tc.tile_pool(name="gpool", bufs=8))
+        cpool = ctx.enter_context(tc.tile_pool(name="cpool", bufs=8))
+        ypool = ctx.enter_context(tc.tile_pool(name="ypool", bufs=8))
         spool = ctx.enter_context(tc.tile_pool(name="spool", bufs=4))
-        tpsum = ctx.enter_context(tc.psum_pool(name="tpsum", bufs=5))
-        opsum = ctx.enter_context(tc.psum_pool(name="opsum", bufs=3))
-        if MANUAL:
-            ctx.enter_context(tc.manual_schedule())
+        tpsum = ctx.enter_context(tc.psum_pool(name="tpsum", bufs=T_BANKS))
+        opsum = ctx.enter_context(tc.psum_pool(name="opsum", bufs=8 - T_BANKS))
+        ctx.enter_context(tc.manual_schedule())
 
         ident_f = const.tile([P, P], F32, name="ident_f")
         ident_b = const.tile([P, P], BF16, name="ident_b")
@@ -55,12 +52,11 @@ def tile_selfattention_pa_kernel(tc, x, W, b, out_0, out_1, out_2):
         w_tiles = {}
 
         def load_w(i):
-            w_sb = wpool.tile([P, 4 * E], BF16, name="w_sb")
-            nc.sync.dma_start(
-                out=w_sb[:],
-                in_=W[512 * i:512 * (i + 1), :].rearrange("(p t) k -> p (t k)", t=4),
-            )
-            w_tiles[i] = w_sb
+            rows = W[512 * i:512 * (i + 1), :].rearrange("(p t) k -> p t k", t=4)
+            for tt in range(2):
+                w_sb = wpool.tile([P, 2, E], BF16, name="w_sb")
+                nc.sync.dma_start(out=w_sb[:], in_=rows[:, 2 * tt:2 * tt + 2, :])
+                w_tiles[(i, tt)] = w_sb
 
         nc.vector.memset(b_sb[:].bitcast(I32), 0)
         nc.vector.memset(warm[:], 1.0)
@@ -68,14 +64,14 @@ def tile_selfattention_pa_kernel(tc, x, W, b, out_0, out_1, out_2):
         for m in range(2):
             for bl in range(2):
                 nc.sync.dma_start(out=x_sb[m][bl:P:2, :], in_=x[2 * m + bl, :, :])
-        for i in range(NW):
+        for i in range(W_AHEAD):
             load_w(i)
         make_identity(nc, ident_b[:])
         make_identity(nc, ident_f[:])
         nc.scalar.sqrt(out=warm2[:], in_=warm[:])
 
-        def drain(eng_is_vector, dst, src):
-            if eng_is_vector:
+        def drain(on_vector, dst, src):
+            if on_vector:
                 nc.vector.tensor_copy(out=dst, in_=src)
             else:
                 nc.scalar.copy(out=dst, in_=src)
@@ -103,9 +99,9 @@ def tile_selfattention_pa_kernel(tc, x, W, b, out_0, out_1, out_2):
                     )
             return tb
 
-        def drain_bank(eng_is_vector, dst32, tb):
+        def drain_bank(on_vector, dst32, tb):
             drain(
-                eng_is_vector,
+                on_vector,
                 dst32.rearrange("q (a c u) -> q a c u", a=2, u=2),
                 tb[:].rearrange("q (a u c) -> q a c u", a=2, u=2),
             )
@@ -125,41 +121,43 @@ def tile_selfattention_pa_kernel(tc, x, W, b, out_0, out_1, out_2):
         acc = {}
         ytile = {}
         stats = {}
+        stored = [0, 0, 0]
 
-        def stage_t(k):
-            i = k // 2
-            w32 = w_tiles[i][:].bitcast(F32)
-            for un in range(2):
-                g = 2 * (k % 2) + un
-                for tt in range(2):
-                    banks[(k, 2 * un + tt)] = transposes_into_bank(
-                        w32, 2 * tt * 1024 + 256 * g, 1024
-                    )
+        def live(i):
+            return 0 <= i < NBLK
 
-        def stage_d(k, j):
-            un = j // 2
-            tt = j % 2
+        def stage_t(i, j):
+            tt = j // 4
+            g = j % 4
+            w32 = w_tiles[(i, tt)][:].rearrange("p t k -> p (t k)").bitcast(F32)
+            banks[(i, j)] = transposes_into_bank(w32, 256 * g, 1024)
+            if j == 7 and live(i + W_AHEAD):
+                load_w(i + W_AHEAD)
+
+        def stage_d(i, j):
+            tt = j // 4
+            g = j % 4
             if tt == 0:
-                grouped[(k, un)] = gpool.tile([P, 2048], BF16, name="grp", align_bytes=64)
-            g32 = grouped[(k, un)][:].bitcast(F32)
-            drain_bank(j in VECTOR_DRAINS, g32[:, 512 * tt:512 * (tt + 1)], banks[(k, j)])
+                grouped[(i, g)] = gpool.tile([P, 2048], BF16, name="grp", align_bytes=64)
+            g32 = grouped[(i, g)][:].bitcast(F32)
+            drain_bank(j >= 6, g32[:, 512 * tt:512 * (tt + 1)], banks[(i, j)])
+            if j + T_BANKS < 8:
+                stage_t(i, j + T_BANKS)
 
-        def stage_q(k, un):
+        def stage_q(i, g):
             cd = cpool.tile([P, 512], U32, name="cd", align_bytes=64)
             sc = cpool.tile([P, 512], U8, name="sc", align_bytes=64)
             nc.vector.quantize_mx(
-                out=cd[:].bitcast(FP8X4), scales=sc[:], in_=grouped[(k, un)][:]
+                out=cd[:].bitcast(FP8X4), scales=sc[:], in_=grouped[(i, g)][:]
             )
-            codes[(k, un)] = (cd, sc)
+            codes[(i, g)] = (cd, sc)
 
-        def stage_m(k):
-            i = k // 2
+        def stage_m(i):
             for m in range(2):
-                if k % 2 == 0:
-                    acc[(i, m)] = opsum.tile([P, 512], F32, name="acc")
-                for un in range(2):
-                    g = 2 * (k % 2) + un
-                    cd, sc = codes[(k, un)]
+                acc[(i, m)] = opsum.tile([P, 512], F32, name="acc")
+            for g in range(NPASS):
+                cd, sc = codes[(i, g)]
+                for m in range(2):
                     xcol = (4 * m + g) * P
                     nc.tensor.matmul_mx(
                         out=acc[(i, m)][:],
@@ -168,7 +166,7 @@ def tile_selfattention_pa_kernel(tc, x, W, b, out_0, out_1, out_2):
                         rhs=cd[:].bitcast(FP8X4),
                         rhs_scale=sc[:],
                         start=(g == 0),
-                        stop=(g == 3),
+                        stop=(g == NPASS - 1),
                     )
 
         def qk_groups(i):
@@ -223,74 +221,70 @@ def tile_selfattention_pa_kernel(tc, x, W, b, out_0, out_1, out_2):
         def stage_scale(i):
             groups = qk_groups(i)
             n = len(groups)
+            eng = nc.vector if i == NBLK - 1 else nc.gpsimd
             for m in range(2):
                 for r in range(n):
                     ap = group_ap(i, m, groups[r])
                     col = m * n + r
-                    rcol = stats[(i, "rn")][:, col:col + 1]
-                    if SCALE_ON_GPSIMD:
-                        nc.gpsimd.tensor_scalar(
-                            out=ap, in0=ap, scalar1=rcol, scalar2=0.0,
-                            op0=ALU.mult, op1=ALU.add,
-                        )
-                    else:
-                        nc.vector.tensor_scalar_mul(out=ap, in0=ap, scalar1=rcol)
-
-        def stage_store(sb):
-            for m in range(2):
-                for bl in range(2):
-                    view = ytile[(sb, m)][bl:P:2, :].rearrange(
-                        "q (h s c) -> q s h c", s=3, c=HD
+                    eng.tensor_scalar(
+                        out=ap, in0=ap, scalar1=stats[(i, "rn")][:, col:col + 1],
+                        scalar2=0.0, op0=ALU.mult, op1=ALU.add,
                     )
-                    for s in range(3):
+
+        def flush(i):
+            sb = i // 3
+            for s in range(3):
+                lo = stored[s]
+                hi = (4 * i + 3 - s) // 3 + 1
+                stored[s] = hi
+                for m in range(2):
+                    for bl in range(2):
+                        view = ytile[(sb, m)][bl:P:2, :].rearrange(
+                            "q (h s c) -> q s h c", s=3, c=HD
+                        )
                         nc.sync.dma_start(
-                            out=outs[s][2 * m + bl, 4 * sb:4 * sb + 4, :, :].rearrange(
-                                "h l c -> l h c"
-                            ),
-                            in_=view[:, s, :, :],
+                            out=outs[s][2 * m + bl, lo:hi, :, :].rearrange("h l c -> l h c"),
+                            in_=view[:, s, lo - 4 * sb:hi - 4 * sb, :],
                         )
 
-        def blk(slot, lag):
-            v = slot - lag
-            if v >= 0 and v % 2 == 0 and v // 2 < NBLK:
-                return v // 2
-            return None
-
-        for k in range(NPAIR + 8):
-            i_rc = blk(k, 7)
-            if i_rc is not None:
-                stage_recip(i_rc)
-                stage_scale(i_rc)
-            i_mx = blk(k, 6)
-            if i_mx is not None:
-                stage_max(i_mx)
-            i_a = blk(k, 4)
-            if i_a is not None:
-                stage_a(i_a, 0)
-                stage_a(i_a, 1)
-            if k < NPAIR:
-                stage_t(k)
-                if k % 2 == 1 and k // 2 + NW < NBLK:
-                    load_w(k // 2 + NW)
+        for i in range(NBLK + 4):
+            if live(i - 3):
+                stage_max(i - 3)
+            if live(i):
+                for j in range(T_BANKS):
+                    stage_t(i, j)
+                stage_d(i, 0)
+            if live(i - 3):
+                stage_sqrt(i - 3)
+            if live(i - 1):
+                stage_q(i - 1, 0)
+            if live(i - 2):
+                stage_a(i - 2, 0)
+            if live(i - 3):
+                stage_recip(i - 3)
+            if live(i - 1):
+                stage_q(i - 1, 1)
+            if live(i - 2):
+                stage_a(i - 2, 1)
+            if live(i - 1):
+                stage_q(i - 1, 2)
+                stage_q(i - 1, 3)
             squares = []
-            if i_a is not None:
-                squares = [(i_a, 0, r) for r in range(len(qk_groups(i_a)))]
-            i_s1 = blk(k, 5)
-            if i_s1 is not None:
-                squares = [(i_s1, 1, r) for r in range(len(qk_groups(i_s1)))]
-            if 1 <= k <= NPAIR:
-                stage_q(k - 1, 0)
-            for j in range(4):
-                if k < NPAIR:
-                    stage_d(k, j)
-                if j < len(squares):
-                    stage_sq(*squares[j])
-            if 1 <= k <= NPAIR:
-                stage_q(k - 1, 1)
-            if i_mx is not None:
-                stage_sqrt(i_mx)
-            if 2 <= k <= NPAIR + 1:
-                stage_m(k - 2)
-            i_st = blk(k, 8)
-            if i_st is not None and i_st % 3 == 2:
-                stage_store(i_st // 3)
+            if live(i - 2):
+                squares = [(i - 2, m, r) for m in range(2) for r in range(len(qk_groups(i - 2)))]
+            for j in range(1, 6):
+                if live(i):
+                    stage_d(i, j)
+                if j - 1 < len(squares):
+                    stage_sq(*squares[j - 1])
+            for sqa in squares[5:]:
+                stage_sq(*sqa)
+            if live(i):
+                stage_d(i, 6)
+                stage_d(i, 7)
+            if live(i - 3):
+                stage_scale(i - 3)
+            if live(i - 1):
+                stage_m(i - 1)
+            if (i - 3) in FLUSH_AFTER:
+                flush(i - 3)

@@ -17,11 +17,12 @@ E = 2048
 NH = 16
 HD = 128
 NBLK = 12
-NPASS = 4
-W_AHEAD = 5
-T_BANKS = 5
-FLUSH_AFTER = (2, 5, 8, 10, 11)
+NPAIR = 24
+NW = 6
 FLOPS = 2 * 256 * 2048 * 6144
+
+FLUSH_AFTER = (2, 5, 8, 10, 11)
+VECTOR_DRAINS = (3,)
 
 
 def tile_selfattention_pa_kernel(tc, x, W, b, out_0, out_1, out_2):
@@ -29,13 +30,13 @@ def tile_selfattention_pa_kernel(tc, x, W, b, out_0, out_1, out_2):
     outs = (out_0, out_1, out_2)
     with ExitStack() as ctx:
         const = ctx.enter_context(tc.tile_pool(name="const", bufs=1))
-        wpool = ctx.enter_context(tc.tile_pool(name="wpool", bufs=2 * W_AHEAD))
-        gpool = ctx.enter_context(tc.tile_pool(name="gpool", bufs=8))
-        cpool = ctx.enter_context(tc.tile_pool(name="cpool", bufs=8))
-        ypool = ctx.enter_context(tc.tile_pool(name="ypool", bufs=8))
+        wpool = ctx.enter_context(tc.tile_pool(name="wpool", bufs=NW))
+        gpool = ctx.enter_context(tc.tile_pool(name="gpool", bufs=6))
+        cpool = ctx.enter_context(tc.tile_pool(name="cpool", bufs=6))
+        ypool = ctx.enter_context(tc.tile_pool(name="ypool", bufs=6))
         spool = ctx.enter_context(tc.tile_pool(name="spool", bufs=4))
-        tpsum = ctx.enter_context(tc.psum_pool(name="tpsum", bufs=T_BANKS))
-        opsum = ctx.enter_context(tc.psum_pool(name="opsum", bufs=8 - T_BANKS))
+        tpsum = ctx.enter_context(tc.psum_pool(name="tpsum", bufs=5))
+        opsum = ctx.enter_context(tc.psum_pool(name="opsum", bufs=3))
         ctx.enter_context(tc.manual_schedule())
 
         ident_f = const.tile([P, P], F32, name="ident_f")
@@ -52,11 +53,16 @@ def tile_selfattention_pa_kernel(tc, x, W, b, out_0, out_1, out_2):
         w_tiles = {}
 
         def load_w(i):
+            w_sb = wpool.tile([P, 4 * E], BF16, name="w_sb")
             rows = W[512 * i:512 * (i + 1), :].rearrange("(p t) k -> p t k", t=4)
-            for tt in range(2):
-                w_sb = wpool.tile([P, 2, E], BF16, name="w_sb")
-                nc.sync.dma_start(out=w_sb[:], in_=rows[:, 2 * tt:2 * tt + 2, :])
-                w_tiles[(i, tt)] = w_sb
+            dst = w_sb[:].rearrange("p (t k) -> p t k", t=4)
+            if i == 0:
+                for half in range(2):
+                    ks = slice(1024 * half, 1024 * (half + 1))
+                    nc.sync.dma_start(out=dst[:, :, ks], in_=rows[:, :, ks])
+            else:
+                nc.sync.dma_start(out=dst, in_=rows)
+            w_tiles[i] = w_sb
 
         nc.vector.memset(b_sb[:].bitcast(I32), 0)
         nc.vector.memset(warm[:], 1.0)
@@ -64,14 +70,14 @@ def tile_selfattention_pa_kernel(tc, x, W, b, out_0, out_1, out_2):
         for m in range(2):
             for bl in range(2):
                 nc.sync.dma_start(out=x_sb[m][bl:P:2, :], in_=x[2 * m + bl, :, :])
-        for i in range(W_AHEAD):
+        for i in range(NW):
             load_w(i)
         make_identity(nc, ident_b[:])
         make_identity(nc, ident_f[:])
         nc.scalar.sqrt(out=warm2[:], in_=warm[:])
 
-        def drain(on_vector, dst, src):
-            if on_vector:
+        def drain(eng_is_vector, dst, src):
+            if eng_is_vector:
                 nc.vector.tensor_copy(out=dst, in_=src)
             else:
                 nc.scalar.copy(out=dst, in_=src)
@@ -99,9 +105,9 @@ def tile_selfattention_pa_kernel(tc, x, W, b, out_0, out_1, out_2):
                     )
             return tb
 
-        def drain_bank(on_vector, dst32, tb):
+        def drain_bank(eng_is_vector, dst32, tb):
             drain(
-                on_vector,
+                eng_is_vector,
                 dst32.rearrange("q (a c u) -> q a c u", a=2, u=2),
                 tb[:].rearrange("q (a u c) -> q a c u", a=2, u=2),
             )
@@ -121,43 +127,41 @@ def tile_selfattention_pa_kernel(tc, x, W, b, out_0, out_1, out_2):
         acc = {}
         ytile = {}
         stats = {}
-        stored = [0, 0, 0]
 
-        def live(i):
-            return 0 <= i < NBLK
+        def stage_t(k):
+            i = k // 2
+            w32 = w_tiles[i][:].bitcast(F32)
+            for un in range(2):
+                g = 2 * (k % 2) + un
+                for tt in range(2):
+                    banks[(k, 2 * un + tt)] = transposes_into_bank(
+                        w32, 2 * tt * 1024 + 256 * g, 1024
+                    )
 
-        def stage_t(i, j):
-            tt = j // 4
-            g = j % 4
-            w32 = w_tiles[(i, tt)][:].rearrange("p t k -> p (t k)").bitcast(F32)
-            banks[(i, j)] = transposes_into_bank(w32, 256 * g, 1024)
-            if j == 7 and live(i + W_AHEAD):
-                load_w(i + W_AHEAD)
-
-        def stage_d(i, j):
-            tt = j // 4
-            g = j % 4
+        def stage_d(k, j):
+            un = j // 2
+            tt = j % 2
             if tt == 0:
-                grouped[(i, g)] = gpool.tile([P, 2048], BF16, name="grp", align_bytes=64)
-            g32 = grouped[(i, g)][:].bitcast(F32)
-            drain_bank(j >= 6, g32[:, 512 * tt:512 * (tt + 1)], banks[(i, j)])
-            if j + T_BANKS < 8:
-                stage_t(i, j + T_BANKS)
+                grouped[(k, un)] = gpool.tile([P, 2048], BF16, name="grp", align_bytes=64)
+            g32 = grouped[(k, un)][:].bitcast(F32)
+            drain_bank(j in VECTOR_DRAINS, g32[:, 512 * tt:512 * (tt + 1)], banks[(k, j)])
 
-        def stage_q(i, g):
+        def stage_q(k, un):
             cd = cpool.tile([P, 512], U32, name="cd", align_bytes=64)
             sc = cpool.tile([P, 512], U8, name="sc", align_bytes=64)
             nc.vector.quantize_mx(
-                out=cd[:].bitcast(FP8X4), scales=sc[:], in_=grouped[(i, g)][:]
+                out=cd[:].bitcast(FP8X4), scales=sc[:], in_=grouped[(k, un)][:]
             )
-            codes[(i, g)] = (cd, sc)
+            codes[(k, un)] = (cd, sc)
 
-        def stage_m(i):
+        def stage_m(k):
+            i = k // 2
             for m in range(2):
-                acc[(i, m)] = opsum.tile([P, 512], F32, name="acc")
-            for g in range(NPASS):
-                cd, sc = codes[(i, g)]
-                for m in range(2):
+                if k % 2 == 0:
+                    acc[(i, m)] = opsum.tile([P, 512], F32, name="acc")
+                for un in range(2):
+                    g = 2 * (k % 2) + un
+                    cd, sc = codes[(k, un)]
                     xcol = (4 * m + g) * P
                     nc.tensor.matmul_mx(
                         out=acc[(i, m)][:],
@@ -166,7 +170,7 @@ def tile_selfattention_pa_kernel(tc, x, W, b, out_0, out_1, out_2):
                         rhs=cd[:].bitcast(FP8X4),
                         rhs_scale=sc[:],
                         start=(g == 0),
-                        stop=(g == NPASS - 1),
+                        stop=(g == 3),
                     )
 
         def qk_groups(i):
@@ -231,9 +235,13 @@ def tile_selfattention_pa_kernel(tc, x, W, b, out_0, out_1, out_2):
                         scalar2=0.0, op0=ALU.mult, op1=ALU.add,
                     )
 
-        def flush(i):
+        stored = [0, 0, 0]
+
+        def flush(i, kinds):
+            if i not in FLUSH_AFTER:
+                return
             sb = i // 3
-            for s in range(3):
+            for s in kinds:
                 lo = stored[s]
                 hi = (4 * i + 3 - s) // 3 + 1
                 stored[s] = hi
@@ -247,44 +255,45 @@ def tile_selfattention_pa_kernel(tc, x, W, b, out_0, out_1, out_2):
                             in_=view[:, s, lo - 4 * sb:hi - 4 * sb, :],
                         )
 
-        for i in range(NBLK + 4):
-            if live(i - 3):
-                stage_max(i - 3)
-            if live(i):
-                for j in range(T_BANKS):
-                    stage_t(i, j)
-                stage_d(i, 0)
-            if live(i - 3):
-                stage_sqrt(i - 3)
-            if live(i - 1):
-                stage_q(i - 1, 0)
-            if live(i - 2):
-                stage_a(i - 2, 0)
-            if live(i - 3):
-                stage_recip(i - 3)
-            if live(i - 1):
-                stage_q(i - 1, 1)
-            if live(i - 2):
-                stage_a(i - 2, 1)
-            if live(i - 1):
-                stage_q(i - 1, 2)
-                stage_q(i - 1, 3)
+        def blk(slot, lag):
+            v = slot - lag
+            if v >= 0 and v % 2 == 0 and v // 2 < NBLK:
+                return v // 2
+            return None
+
+        for k in range(NPAIR + 8):
+            i_rc = blk(k, 7)
+            if i_rc is not None:
+                stage_recip(i_rc)
+                stage_scale(i_rc)
+                flush(i_rc, (0, 1))
+            i_mx = blk(k, 6)
+            if i_mx is not None:
+                stage_max(i_mx)
+            i_a = blk(k, 4)
+            if i_a is not None:
+                stage_a(i_a, 0)
+                stage_a(i_a, 1)
+                flush(i_a, (2,))
+            if k < NPAIR:
+                stage_t(k)
+                if k % 2 == 1 and k // 2 + NW < NBLK:
+                    load_w(k // 2 + NW)
             squares = []
-            if live(i - 2):
-                squares = [(i - 2, m, r) for m in range(2) for r in range(len(qk_groups(i - 2)))]
-            for j in range(1, 6):
-                if live(i):
-                    stage_d(i, j)
-                if j - 1 < len(squares):
-                    stage_sq(*squares[j - 1])
-            for sqa in squares[5:]:
-                stage_sq(*sqa)
-            if live(i):
-                stage_d(i, 6)
-                stage_d(i, 7)
-            if live(i - 3):
-                stage_scale(i - 3)
-            if live(i - 1):
-                stage_m(i - 1)
-            if (i - 3) in FLUSH_AFTER:
-                flush(i - 3)
+            if i_a is not None:
+                squares = [(i_a, 0, r) for r in range(len(qk_groups(i_a)))]
+            i_s1 = blk(k, 5)
+            if i_s1 is not None:
+                squares = [(i_s1, 1, r) for r in range(len(qk_groups(i_s1)))]
+            if 1 <= k <= NPAIR:
+                stage_q(k - 1, 0)
+                stage_q(k - 1, 1)
+            for j in range(4):
+                if k < NPAIR:
+                    stage_d(k, j)
+                if j < len(squares):
+                    stage_sq(*squares[j])
+            if i_mx is not None:
+                stage_sqrt(i_mx)
+            if 2 <= k <= NPAIR + 1:
+                stage_m(k - 2)

@@ -33,7 +33,7 @@ def tile_selfattention_pa_kernel(tc, x, W, b, out_0, out_1, out_2):
         wpool = ctx.enter_context(tc.tile_pool(name="wpool", bufs=NW))
         gpool = ctx.enter_context(tc.tile_pool(name="gpool", bufs=6))
         cpool = ctx.enter_context(tc.tile_pool(name="cpool", bufs=6))
-        ypool = ctx.enter_context(tc.tile_pool(name="ypool", bufs=6))
+        ypool = ctx.enter_context(tc.tile_pool(name="ypool", bufs=4))
         spool = ctx.enter_context(tc.tile_pool(name="spool", bufs=4))
         tpsum = ctx.enter_context(tc.psum_pool(name="tpsum", bufs=5))
         opsum = ctx.enter_context(tc.psum_pool(name="opsum", bufs=3))
@@ -45,7 +45,7 @@ def tile_selfattention_pa_kernel(tc, x, W, b, out_0, out_1, out_2):
         bias_bc = const.tile([P, 6144], BF16, name="bias_bc")
         warm = const.tile([P, 1], F32, name="warm")
         warm2 = const.tile([P, 1], F32, name="warm2")
-        x_sb = [const.tile([P, E], BF16, name="x_sb%d" % m) for m in range(2)]
+        x_sb = const.tile([P, 2, E], BF16, name="x_sb")
         xg = const.tile([P, 4096], BF16, name="xg", align_bytes=64)
         xc = const.tile([P, 1024], U32, name="xc", align_bytes=64)
         xs = const.tile([P, 1024], U8, name="xs", align_bytes=64)
@@ -67,9 +67,11 @@ def tile_selfattention_pa_kernel(tc, x, W, b, out_0, out_1, out_2):
         nc.vector.memset(b_sb[:].bitcast(I32), 0)
         nc.vector.memset(warm[:], 1.0)
         nc.sync.dma_start(out=b_sb[0:16, :], in_=b.rearrange("(h n) -> h n", h=16))
-        for m in range(2):
-            for bl in range(2):
-                nc.sync.dma_start(out=x_sb[m][bl:P:2, :], in_=x[2 * m + bl, :, :])
+        for bi in range(4):
+            nc.sync.dma_start(
+                out=x_sb[bi:P:4, :, :],
+                in_=x[bi, :, :].rearrange("(lh m) k -> lh m k", m=2),
+            )
         for i in range(NW):
             load_w(i)
         make_identity(nc, ident_b[:])
@@ -113,10 +115,10 @@ def tile_selfattention_pa_kernel(tc, x, W, b, out_0, out_1, out_2):
             )
 
         xg32 = xg[:].bitcast(F32)
+        x32 = x_sb[:].rearrange("p m k -> p (m k)").bitcast(F32)
         for m in range(2):
-            x32 = x_sb[m][:].bitcast(F32)
             for gp in range(2):
-                tb = transposes_into_bank(x32, 512 * gp, 256)
+                tb = transposes_into_bank(x32, 1024 * m + 512 * gp, 256)
                 w0 = (4 * m + 2 * gp) * 256
                 drain_bank(gp == 0, xg32[:, w0:w0 + 512], tb)
         nc.vector.quantize_mx(out=xc[:].bitcast(FP8X4), scales=xs[:], in_=xg[:])
@@ -176,20 +178,24 @@ def tile_selfattention_pa_kernel(tc, x, W, b, out_0, out_1, out_2):
         def qk_groups(i):
             return [gq for gq in range(4) if (4 * i + gq) % 3 != 2]
 
+        def y_view(sb):
+            return ytile[sb][:].rearrange("q (n m c) -> q n m c", m=2, c=HD)
+
         def stage_a(i, m):
-            if i % 3 == 0:
-                ytile[(i // 3, m)] = ypool.tile([P, 1536], F32, name="y3")
-            off = 512 * (i % 3)
+            if i % 3 == 0 and m == 0:
+                ytile[i // 3] = ypool.tile([P, 3072], F32, name="y3")
+            n0 = 4 * (i % 3)
             nc.vector.tensor_tensor(
-                out=ytile[(i // 3, m)][:, off:off + 512].rearrange("q (p t) -> q p t", t=4),
-                in0=acc[(i, m)][:].rearrange("q (t p) -> q p t", t=4),
-                in1=bias_bc[:, 512 * i:512 * (i + 1)].rearrange("q (p t) -> q p t", t=4),
+                out=y_view(i // 3)[:, n0:n0 + 4, m, :].rearrange("q n (r t) -> q n r t", t=4),
+                in0=acc[(i, m)][:].rearrange("q (t n r) -> q n r t", t=4, n=4),
+                in1=bias_bc[:, 512 * i:512 * (i + 1)].rearrange(
+                    "q (n r t) -> q n r t", n=4, t=4
+                ),
                 op=ALU.add,
             )
 
         def group_ap(i, m, gq):
-            off = 512 * (i % 3) + P * gq
-            return ytile[(i // 3, m)][:, off:off + P]
+            return y_view(i // 3)[:, 4 * (i % 3) + gq, m, :]
 
         def stage_sq(i, m, r):
             groups = qk_groups(i)
@@ -245,15 +251,16 @@ def tile_selfattention_pa_kernel(tc, x, W, b, out_0, out_1, out_2):
                 lo = stored[s]
                 hi = (4 * i + 3 - s) // 3 + 1
                 stored[s] = hi
-                for m in range(2):
-                    for bl in range(2):
-                        view = ytile[(sb, m)][bl:P:2, :].rearrange(
-                            "q (h s c) -> q s h c", s=3, c=HD
-                        )
-                        nc.sync.dma_start(
-                            out=outs[s][2 * m + bl, lo:hi, :, :].rearrange("h l c -> l h c"),
-                            in_=view[:, s, lo - 4 * sb:hi - 4 * sb, :],
-                        )
+                for bi in range(4):
+                    view = ytile[sb][bi:P:4, :].rearrange(
+                        "q (h s f) -> q s h f", s=3, f=2 * HD
+                    )
+                    nc.sync.dma_start(
+                        out=outs[s][bi, lo:hi, :, :].rearrange(
+                            "h (lh m) c -> lh h (m c)", m=2
+                        ),
+                        in_=view[:, s, lo - 4 * sb:hi - 4 * sb, :],
+                    )
 
         def blk(slot, lag):
             v = slot - lag

@@ -33,7 +33,7 @@ def tile_selfattention_pa_kernel(tc, x, W, b, out_0, out_1, out_2):
         wpool = ctx.enter_context(tc.tile_pool(name="wpool", bufs=NW))
         gpool = ctx.enter_context(tc.tile_pool(name="gpool", bufs=6))
         cpool = ctx.enter_context(tc.tile_pool(name="cpool", bufs=6))
-        ypool = ctx.enter_context(tc.tile_pool(name="ypool", bufs=4))
+        ypool = ctx.enter_context(tc.tile_pool(name="ypool", bufs=6))
         spool = ctx.enter_context(tc.tile_pool(name="spool", bufs=4))
         tpsum = ctx.enter_context(tc.psum_pool(name="tpsum", bufs=5))
         opsum = ctx.enter_context(tc.psum_pool(name="opsum", bufs=3))
@@ -45,37 +45,37 @@ def tile_selfattention_pa_kernel(tc, x, W, b, out_0, out_1, out_2):
         bias_bc = const.tile([P, 6144], BF16, name="bias_bc")
         warm = const.tile([P, 1], F32, name="warm")
         warm2 = const.tile([P, 1], F32, name="warm2")
-        x_sb = const.tile([P, 2, E], BF16, name="x_sb")
+        x_sb = [const.tile([P, E], BF16, name="x_sb%d" % m) for m in range(2)]
         xg = const.tile([P, 4096], BF16, name="xg", align_bytes=64)
         xc = const.tile([P, 1024], U32, name="xc", align_bytes=64)
         xs = const.tile([P, 1024], U8, name="xs", align_bytes=64)
 
         w_tiles = {}
+        w_words = W.bitcast(F32)
 
         def load_w(i):
             w_sb = wpool.tile([P, 4 * E], BF16, name="w_sb")
-            rows = W[512 * i:512 * (i + 1), :].rearrange("(p t) k -> p t k", t=4)
-            dst = w_sb[:].rearrange("p (t k) -> p t k", t=4)
+            rows = w_words[512 * i:512 * (i + 1), :].rearrange("(p t) k -> p t k", t=4)
+            dst = w_sb[:].bitcast(F32).rearrange("p (t k) -> p t k", t=4)
             if i == 0:
                 for half in range(2):
-                    ks = slice(1024 * half, 1024 * (half + 1))
-                    nc.sync.dma_start(out=dst[:, :, ks], in_=rows[:, :, ks])
+                    ks = slice(512 * half, 512 * (half + 1))
+                    nc.gpsimd.dma_start(out=dst[:, :, ks], in_=rows[:, :, ks])
             else:
-                nc.sync.dma_start(out=dst, in_=rows)
+                nc.gpsimd.dma_start(out=dst, in_=rows)
             w_tiles[i] = w_sb
 
         nc.vector.memset(b_sb[:].bitcast(I32), 0)
         nc.vector.memset(warm[:], 1.0)
         nc.sync.dma_start(out=b_sb[0:16, :], in_=b.rearrange("(h n) -> h n", h=16))
-        for bi in range(4):
-            nc.sync.dma_start(
-                out=x_sb[bi:P:4, :, :],
-                in_=x[bi, :, :].rearrange("(lh m) k -> lh m k", m=2),
-            )
-        for i in range(NW):
-            load_w(i)
+        for m in range(2):
+            for bl in range(2):
+                nc.sync.dma_start(out=x_sb[m][bl:P:2, :], in_=x[2 * m + bl, :, :])
+        load_w(0)
         make_identity(nc, ident_b[:])
         make_identity(nc, ident_f[:])
+        for i in range(1, NW):
+            load_w(i)
         nc.scalar.sqrt(out=warm2[:], in_=warm[:])
 
         def drain(eng_is_vector, dst, src):
@@ -115,10 +115,10 @@ def tile_selfattention_pa_kernel(tc, x, W, b, out_0, out_1, out_2):
             )
 
         xg32 = xg[:].bitcast(F32)
-        x32 = x_sb[:].rearrange("p m k -> p (m k)").bitcast(F32)
         for m in range(2):
+            x32 = x_sb[m][:].bitcast(F32)
             for gp in range(2):
-                tb = transposes_into_bank(x32, 1024 * m + 512 * gp, 256)
+                tb = transposes_into_bank(x32, 512 * gp, 256)
                 w0 = (4 * m + 2 * gp) * 256
                 drain_bank(gp == 0, xg32[:, w0:w0 + 512], tb)
         nc.vector.quantize_mx(out=xc[:].bitcast(FP8X4), scales=xs[:], in_=xg[:])
@@ -178,24 +178,20 @@ def tile_selfattention_pa_kernel(tc, x, W, b, out_0, out_1, out_2):
         def qk_groups(i):
             return [gq for gq in range(4) if (4 * i + gq) % 3 != 2]
 
-        def y_view(sb):
-            return ytile[sb][:].rearrange("q (n m c) -> q n m c", m=2, c=HD)
-
         def stage_a(i, m):
-            if i % 3 == 0 and m == 0:
-                ytile[i // 3] = ypool.tile([P, 3072], F32, name="y3")
-            n0 = 4 * (i % 3)
+            if i % 3 == 0:
+                ytile[(i // 3, m)] = ypool.tile([P, 1536], F32, name="y3")
+            off = 512 * (i % 3)
             nc.vector.tensor_tensor(
-                out=y_view(i // 3)[:, n0:n0 + 4, m, :].rearrange("q n (r t) -> q n r t", t=4),
-                in0=acc[(i, m)][:].rearrange("q (t n r) -> q n r t", t=4, n=4),
-                in1=bias_bc[:, 512 * i:512 * (i + 1)].rearrange(
-                    "q (n r t) -> q n r t", n=4, t=4
-                ),
+                out=ytile[(i // 3, m)][:, off:off + 512].rearrange("q (p t) -> q p t", t=4),
+                in0=acc[(i, m)][:].rearrange("q (t p) -> q p t", t=4),
+                in1=bias_bc[:, 512 * i:512 * (i + 1)].rearrange("q (p t) -> q p t", t=4),
                 op=ALU.add,
             )
 
         def group_ap(i, m, gq):
-            return y_view(i // 3)[:, 4 * (i % 3) + gq, m, :]
+            off = 512 * (i % 3) + P * gq
+            return ytile[(i // 3, m)][:, off:off + P]
 
         def stage_sq(i, m, r):
             groups = qk_groups(i)
@@ -251,16 +247,15 @@ def tile_selfattention_pa_kernel(tc, x, W, b, out_0, out_1, out_2):
                 lo = stored[s]
                 hi = (4 * i + 3 - s) // 3 + 1
                 stored[s] = hi
-                for bi in range(4):
-                    view = ytile[sb][bi:P:4, :].rearrange(
-                        "q (h s f) -> q s h f", s=3, f=2 * HD
-                    )
-                    nc.sync.dma_start(
-                        out=outs[s][bi, lo:hi, :, :].rearrange(
-                            "h (lh m) c -> lh h (m c)", m=2
-                        ),
-                        in_=view[:, s, lo - 4 * sb:hi - 4 * sb, :],
-                    )
+                for m in range(2):
+                    for bl in range(2):
+                        view = ytile[(sb, m)][bl:P:2, :].rearrange(
+                            "q (h s c) -> q s h c", s=3, c=HD
+                        )
+                        nc.sync.dma_start(
+                            out=outs[s][2 * m + bl, lo:hi, :, :].rearrange("h l c -> l h c"),
+                            in_=view[:, s, lo - 4 * sb:hi - 4 * sb, :],
+                        )
 
         def blk(slot, lag):
             v = slot - lag

@@ -21,7 +21,7 @@ NPAIR = 24
 NW = 6
 FLOPS = 2 * 256 * 2048 * 6144
 
-FLUSH_AFTER = (2, 5, 8, 10, 11)
+SPLIT_LOADS = 4
 VECTOR_DRAINS = (3,)
 
 
@@ -51,18 +51,17 @@ def tile_selfattention_pa_kernel(tc, x, W, b, out_0, out_1, out_2):
         xs = const.tile([P, 1024], U8, name="xs", align_bytes=64)
 
         w_tiles = {}
-        w_words = W.bitcast(F32)
 
         def load_w(i):
             w_sb = wpool.tile([P, 4 * E], BF16, name="w_sb")
-            rows = w_words[512 * i:512 * (i + 1), :].rearrange("(p t) k -> p t k", t=4)
-            dst = w_sb[:].bitcast(F32).rearrange("p (t k) -> p t k", t=4)
-            if i == 0:
+            rows = W[512 * i:512 * (i + 1), :].rearrange("(p t) k -> p t k", t=4)
+            dst = w_sb[:].rearrange("p (t k) -> p t k", t=4)
+            if i < SPLIT_LOADS:
                 for half in range(2):
-                    ks = slice(512 * half, 512 * (half + 1))
-                    nc.gpsimd.dma_start(out=dst[:, :, ks], in_=rows[:, :, ks])
+                    ks = slice(1024 * half, 1024 * (half + 1))
+                    nc.sync.dma_start(out=dst[:, :, ks], in_=rows[:, :, ks])
             else:
-                nc.gpsimd.dma_start(out=dst, in_=rows)
+                nc.sync.dma_start(out=dst, in_=rows)
             w_tiles[i] = w_sb
 
         nc.vector.memset(b_sb[:].bitcast(I32), 0)
@@ -71,11 +70,10 @@ def tile_selfattention_pa_kernel(tc, x, W, b, out_0, out_1, out_2):
         for m in range(2):
             for bl in range(2):
                 nc.sync.dma_start(out=x_sb[m][bl:P:2, :], in_=x[2 * m + bl, :, :])
-        load_w(0)
+        for i in range(NW):
+            load_w(i)
         make_identity(nc, ident_b[:])
         make_identity(nc, ident_f[:])
-        for i in range(1, NW):
-            load_w(i)
         nc.scalar.sqrt(out=warm2[:], in_=warm[:])
 
         def drain(eng_is_vector, dst, src):
@@ -227,7 +225,7 @@ def tile_selfattention_pa_kernel(tc, x, W, b, out_0, out_1, out_2):
         def stage_scale(i):
             groups = qk_groups(i)
             n = len(groups)
-            eng = nc.vector if i == NBLK - 1 else nc.gpsimd
+            eng = nc.vector if i >= NBLK - 2 else nc.gpsimd
             for m in range(2):
                 for r in range(n):
                     ap = group_ap(i, m, groups[r])
@@ -237,24 +235,21 @@ def tile_selfattention_pa_kernel(tc, x, W, b, out_0, out_1, out_2):
                         scalar2=0.0, op0=ALU.mult, op1=ALU.add,
                     )
 
-        stored = [0, 0, 0]
-
         def flush(i, kinds):
-            if i not in FLUSH_AFTER:
+            if i % 3 != 2:
                 return
             sb = i // 3
             for s in kinds:
-                lo = stored[s]
-                hi = (4 * i + 3 - s) // 3 + 1
-                stored[s] = hi
                 for m in range(2):
                     for bl in range(2):
                         view = ytile[(sb, m)][bl:P:2, :].rearrange(
                             "q (h s c) -> q s h c", s=3, c=HD
                         )
                         nc.sync.dma_start(
-                            out=outs[s][2 * m + bl, lo:hi, :, :].rearrange("h l c -> l h c"),
-                            in_=view[:, s, lo - 4 * sb:hi - 4 * sb, :],
+                            out=outs[s][2 * m + bl, 4 * sb:4 * sb + 4, :, :].rearrange(
+                                "h l c -> l h c"
+                            ),
+                            in_=view[:, s, :, :],
                         )
 
         def blk(slot, lag):

@@ -17,12 +17,10 @@ E = 2048
 NH = 16
 HD = 128
 NBLK = 12
-NPAIR = 24
-NW = 6
+NSLOT = 2 * NBLK
+W_AHEAD = 12
+T_BANKS = 5
 FLOPS = 2 * 256 * 2048 * 6144
-
-SPLIT_LOADS = 4
-VECTOR_DRAINS = (3,)
 
 
 def tile_selfattention_pa_kernel(tc, x, W, b, out_0, out_1, out_2):
@@ -30,13 +28,13 @@ def tile_selfattention_pa_kernel(tc, x, W, b, out_0, out_1, out_2):
     outs = (out_0, out_1, out_2)
     with ExitStack() as ctx:
         const = ctx.enter_context(tc.tile_pool(name="const", bufs=1))
-        wpool = ctx.enter_context(tc.tile_pool(name="wpool", bufs=NW))
-        gpool = ctx.enter_context(tc.tile_pool(name="gpool", bufs=6))
+        wpool = ctx.enter_context(tc.tile_pool(name="wpool", bufs=W_AHEAD))
+        gpool = ctx.enter_context(tc.tile_pool(name="gpool", bufs=8))
         cpool = ctx.enter_context(tc.tile_pool(name="cpool", bufs=6))
         ypool = ctx.enter_context(tc.tile_pool(name="ypool", bufs=6))
         spool = ctx.enter_context(tc.tile_pool(name="spool", bufs=4))
-        tpsum = ctx.enter_context(tc.psum_pool(name="tpsum", bufs=5))
-        opsum = ctx.enter_context(tc.psum_pool(name="opsum", bufs=3))
+        tpsum = ctx.enter_context(tc.psum_pool(name="tpsum", bufs=T_BANKS))
+        opsum = ctx.enter_context(tc.psum_pool(name="opsum", bufs=8 - T_BANKS))
         ctx.enter_context(tc.manual_schedule())
 
         ident_f = const.tile([P, P], F32, name="ident_f")
@@ -52,17 +50,13 @@ def tile_selfattention_pa_kernel(tc, x, W, b, out_0, out_1, out_2):
 
         w_tiles = {}
 
-        def load_w(i):
-            w_sb = wpool.tile([P, 4 * E], BF16, name="w_sb")
-            rows = W[512 * i:512 * (i + 1), :].rearrange("(p t) k -> p t k", t=4)
-            dst = w_sb[:].rearrange("p (t k) -> p t k", t=4)
-            if i < SPLIT_LOADS:
-                for half in range(2):
-                    ks = slice(1024 * half, 1024 * (half + 1))
-                    nc.sync.dma_start(out=dst[:, :, ks], in_=rows[:, :, ks])
-            else:
-                nc.sync.dma_start(out=dst, in_=rows)
-            w_tiles[i] = w_sb
+        def load_w(k):
+            blk = k // 2
+            tt = k % 2
+            rows = W[512 * blk:512 * (blk + 1), :].rearrange("(p t) k -> p t k", t=4)
+            w_sb = wpool.tile([P, 2, E], BF16, name="w_sb")
+            nc.sync.dma_start(out=w_sb[:], in_=rows[:, 2 * tt:2 * tt + 2, :])
+            w_tiles[k] = w_sb
 
         nc.vector.memset(b_sb[:].bitcast(I32), 0)
         nc.vector.memset(warm[:], 1.0)
@@ -70,14 +64,14 @@ def tile_selfattention_pa_kernel(tc, x, W, b, out_0, out_1, out_2):
         for m in range(2):
             for bl in range(2):
                 nc.sync.dma_start(out=x_sb[m][bl:P:2, :], in_=x[2 * m + bl, :, :])
-        for i in range(NW):
-            load_w(i)
+        for k in range(W_AHEAD):
+            load_w(k)
         make_identity(nc, ident_b[:])
         make_identity(nc, ident_f[:])
         nc.scalar.sqrt(out=warm2[:], in_=warm[:])
 
-        def drain(eng_is_vector, dst, src):
-            if eng_is_vector:
+        def drain(on_vector, dst, src):
+            if on_vector:
                 nc.vector.tensor_copy(out=dst, in_=src)
             else:
                 nc.scalar.copy(out=dst, in_=src)
@@ -105,9 +99,9 @@ def tile_selfattention_pa_kernel(tc, x, W, b, out_0, out_1, out_2):
                     )
             return tb
 
-        def drain_bank(eng_is_vector, dst32, tb):
+        def drain_bank(on_vector, dst32, tb):
             drain(
-                eng_is_vector,
+                on_vector,
                 dst32.rearrange("q (a c u) -> q a c u", a=2, u=2),
                 tb[:].rearrange("q (a u c) -> q a c u", a=2, u=2),
             )
@@ -129,42 +123,37 @@ def tile_selfattention_pa_kernel(tc, x, W, b, out_0, out_1, out_2):
         stats = {}
 
         def stage_t(k):
-            i = k // 2
-            w32 = w_tiles[i][:].bitcast(F32)
-            for un in range(2):
-                g = 2 * (k % 2) + un
-                for tt in range(2):
-                    banks[(k, 2 * un + tt)] = transposes_into_bank(
-                        w32, 2 * tt * 1024 + 256 * g, 1024
-                    )
+            w32 = w_tiles[k][:].rearrange("p t k -> p (t k)").bitcast(F32)
+            for g in range(4):
+                banks[(k, g)] = transposes_into_bank(w32, 256 * g, 1024)
+            if k + W_AHEAD < NSLOT:
+                load_w(k + W_AHEAD)
 
-        def stage_d(k, j):
-            un = j // 2
-            tt = j % 2
+        def stage_d(k, g):
+            blk = k // 2
+            tt = k % 2
             if tt == 0:
-                grouped[(k, un)] = gpool.tile([P, 2048], BF16, name="grp", align_bytes=64)
-            g32 = grouped[(k, un)][:].bitcast(F32)
-            drain_bank(j in VECTOR_DRAINS, g32[:, 512 * tt:512 * (tt + 1)], banks[(k, j)])
+                grouped[(blk, g)] = gpool.tile([P, 2048], BF16, name="grp", align_bytes=64)
+            g32 = grouped[(blk, g)][:].bitcast(F32)
+            drain_bank(g == 3, g32[:, 512 * tt:512 * (tt + 1)], banks[(k, g)])
 
-        def stage_q(k, un):
+        def stage_q(blk, g):
             cd = cpool.tile([P, 512], U32, name="cd", align_bytes=64)
             sc = cpool.tile([P, 512], U8, name="sc", align_bytes=64)
             nc.vector.quantize_mx(
-                out=cd[:].bitcast(FP8X4), scales=sc[:], in_=grouped[(k, un)][:]
+                out=cd[:].bitcast(FP8X4), scales=sc[:], in_=grouped[(blk, g)][:]
             )
-            codes[(k, un)] = (cd, sc)
+            codes[(blk, g)] = (cd, sc)
 
-        def stage_m(k):
-            i = k // 2
+        def stage_m(blk, gp):
             for m in range(2):
-                if k % 2 == 0:
-                    acc[(i, m)] = opsum.tile([P, 512], F32, name="acc")
-                for un in range(2):
-                    g = 2 * (k % 2) + un
-                    cd, sc = codes[(k, un)]
+                if gp == 0:
+                    acc[(blk, m)] = opsum.tile([P, 512], F32, name="acc")
+                for g in (2 * gp, 2 * gp + 1):
+                    cd, sc = codes[(blk, g)]
                     xcol = (4 * m + g) * P
                     nc.tensor.matmul_mx(
-                        out=acc[(i, m)][:],
+                        out=acc[(blk, m)][:],
                         lhsT=xc[:, xcol:xcol + P].bitcast(FP8X4),
                         lhsT_scale=xs[:, xcol:xcol + P],
                         rhs=cd[:].bitcast(FP8X4),
@@ -252,45 +241,43 @@ def tile_selfattention_pa_kernel(tc, x, W, b, out_0, out_1, out_2):
                             in_=view[:, s, :, :],
                         )
 
-        def blk(slot, lag):
+        def block_at(slot, lag):
             v = slot - lag
             if v >= 0 and v % 2 == 0 and v // 2 < NBLK:
                 return v // 2
             return None
 
-        for k in range(NPAIR + 8):
-            i_rc = blk(k, 7)
+        for k in range(NSLOT + 9):
+            i_rc = block_at(k, 8)
             if i_rc is not None:
                 stage_recip(i_rc)
                 stage_scale(i_rc)
                 flush(i_rc, (0, 1))
-            i_mx = blk(k, 6)
+            i_mx = block_at(k, 7)
             if i_mx is not None:
                 stage_max(i_mx)
-            i_a = blk(k, 4)
+            i_a = block_at(k, 5)
             if i_a is not None:
                 stage_a(i_a, 0)
                 stage_a(i_a, 1)
                 flush(i_a, (2,))
-            if k < NPAIR:
+            if k < NSLOT:
                 stage_t(k)
-                if k % 2 == 1 and k // 2 + NW < NBLK:
-                    load_w(k // 2 + NW)
             squares = []
             if i_a is not None:
                 squares = [(i_a, 0, r) for r in range(len(qk_groups(i_a)))]
-            i_s1 = blk(k, 5)
+            i_s1 = block_at(k, 6)
             if i_s1 is not None:
                 squares = [(i_s1, 1, r) for r in range(len(qk_groups(i_s1)))]
-            if 1 <= k <= NPAIR:
-                stage_q(k - 1, 0)
-                stage_q(k - 1, 1)
+            if 0 <= k - 2 < NSLOT:
+                stage_q((k - 2) // 2, 2 * (k % 2))
+                stage_q((k - 2) // 2, 2 * (k % 2) + 1)
             for j in range(4):
-                if k < NPAIR:
+                if k < NSLOT:
                     stage_d(k, j)
                 if j < len(squares):
                     stage_sq(*squares[j])
             if i_mx is not None:
                 stage_sqrt(i_mx)
-            if 2 <= k <= NPAIR + 1:
-                stage_m(k - 2)
+            if 0 <= k - 3 < NSLOT:
+                stage_m((k - 3) // 2, (k - 3) % 2)

@@ -14,12 +14,13 @@ ACT = mybir.ActivationFunctionType
 
 P = 128
 E = 2048
-NH = 16
+HEADS = 16
 HD = 128
-NBLK = 12
-NSLOT = 2 * NBLK
+PASSES = 4
+BLOCKS = 12
+SLOTS = 2 * BLOCKS
 W_AHEAD = 12
-T_BANKS = 5
+T_BANKS = 6
 FLOPS = 2 * 256 * 2048 * 6144
 
 
@@ -39,245 +40,250 @@ def tile_selfattention_pa_kernel(tc, x, W, b, out_0, out_1, out_2):
 
         ident_f = const.tile([P, P], F32, name="ident_f")
         ident_b = const.tile([P, P], BF16, name="ident_b")
-        b_sb = const.tile([P, 384], BF16, name="b_sb")
-        bias_bc = const.tile([P, 6144], BF16, name="bias_bc")
-        warm = const.tile([P, 1], F32, name="warm")
-        warm2 = const.tile([P, 1], F32, name="warm2")
+        b_rows = const.tile([P, 384], BF16, name="b_sb")
+        bias_all = const.tile([P, 6144], BF16, name="bias_bc")
+        one = const.tile([P, 1], F32, name="warm")
+        one_root = const.tile([P, 1], F32, name="warm2")
         x_sb = [const.tile([P, E], BF16, name="x_sb%d" % m) for m in range(2)]
-        xg = const.tile([P, 4096], BF16, name="xg", align_bytes=64)
-        xc = const.tile([P, 1024], U32, name="xc", align_bytes=64)
-        xs = const.tile([P, 1024], U8, name="xs", align_bytes=64)
+        x_grouped = const.tile([P, 4096], BF16, name="xg", align_bytes=64)
+        x_words = const.tile([P, 1024], U32, name="xc", align_bytes=64)
+        x_scales = const.tile([P, 1024], U8, name="xs", align_bytes=64)
 
-        w_tiles = {}
+        w_half = {}
 
-        def load_w(k):
-            blk = k // 2
-            tt = k % 2
-            rows = W[512 * blk:512 * (blk + 1), :].rearrange("(p t) k -> p t k", t=4)
+        def load_w(slot):
+            block, tt = slot // 2, slot % 2
+            rows = W[512 * block:512 * (block + 1), :].rearrange("(p t) k -> p t k", t=4)
             w_sb = wpool.tile([P, 2, E], BF16, name="w_sb")
             nc.sync.dma_start(out=w_sb[:], in_=rows[:, 2 * tt:2 * tt + 2, :])
-            w_tiles[k] = w_sb
+            w_half[slot] = w_sb
 
-        nc.vector.memset(b_sb[:].bitcast(I32), 0)
-        nc.vector.memset(warm[:], 1.0)
-        nc.sync.dma_start(out=b_sb[0:16, :], in_=b.rearrange("(h n) -> h n", h=16))
+        nc.vector.memset(b_rows[:].bitcast(I32), 0)
+        nc.vector.memset(one[:], 1.0)
+        nc.sync.dma_start(out=b_rows[0:16, :], in_=b.rearrange("(h n) -> h n", h=16))
         for m in range(2):
             for bl in range(2):
                 nc.sync.dma_start(out=x_sb[m][bl:P:2, :], in_=x[2 * m + bl, :, :])
-        for k in range(W_AHEAD):
-            load_w(k)
+        for slot in range(W_AHEAD):
+            load_w(slot)
         make_identity(nc, ident_b[:])
         make_identity(nc, ident_f[:])
-        nc.scalar.sqrt(out=warm2[:], in_=warm[:])
+        nc.scalar.sqrt(out=one_root[:], in_=one[:])
 
-        def drain(on_vector, dst, src):
+        def copy_out(on_vector, dst, src):
             if on_vector:
                 nc.vector.tensor_copy(out=dst, in_=src)
             else:
                 nc.scalar.copy(out=dst, in_=src)
 
-        for h in range(NH):
-            tb = tpsum.tile([P, 512], F32, name="tb")
+        for h in range(HEADS):
+            bank = tpsum.tile([P, 512], F32, name="tb")
             nc.tensor.matmul(
-                out=tb[:, 0:384],
+                out=bank[:, 0:384],
                 lhsT=ident_b[:, h:h + 1].to_broadcast([P, P]),
-                rhs=b_sb[:],
+                rhs=b_rows[:],
                 start=True,
                 stop=True,
             )
-            drain(h % 2 == 0, bias_bc[:, 384 * h:384 * (h + 1)], tb[:, 0:384])
+            copy_out(h % 2 == 0, bias_all[:, 384 * h:384 * (h + 1)], bank[:, 0:384])
 
-        def transposes_into_bank(src32, col0, step_a):
-            tb = tpsum.tile([P, 512], F32, name="tb")
+        def transpose_four(words, first, step):
+            bank = tpsum.tile([P, 512], F32, name="tb")
             for a in range(2):
                 for u in range(2):
-                    c0 = col0 + a * step_a + 128 * u
+                    c0 = first + a * step + 128 * u
                     nc.tensor.transpose(
-                        out=tb[:, (2 * a + u) * P:(2 * a + u + 1) * P],
-                        in_=src32[:, c0:c0 + P],
+                        out=bank[:, (2 * a + u) * P:(2 * a + u + 1) * P],
+                        in_=words[:, c0:c0 + P],
                         identity=ident_f[:],
                     )
-            return tb
+            return bank
 
-        def drain_bank(on_vector, dst32, tb):
-            drain(
+        def regroup(on_vector, dst_words, bank):
+            copy_out(
                 on_vector,
-                dst32.rearrange("q (a c u) -> q a c u", a=2, u=2),
-                tb[:].rearrange("q (a u c) -> q a c u", a=2, u=2),
+                dst_words.rearrange("p (a c u) -> p a c u", a=2, u=2),
+                bank[:].rearrange("p (a u c) -> p a c u", a=2, u=2),
             )
 
-        xg32 = xg[:].bitcast(F32)
+        x_grouped_words = x_grouped[:].bitcast(F32)
         for m in range(2):
-            x32 = x_sb[m][:].bitcast(F32)
-            for gp in range(2):
-                tb = transposes_into_bank(x32, 512 * gp, 256)
-                w0 = (4 * m + 2 * gp) * 256
-                drain_bank(gp == 0, xg32[:, w0:w0 + 512], tb)
-        nc.vector.quantize_mx(out=xc[:].bitcast(FP8X4), scales=xs[:], in_=xg[:])
+            x_in_words = x_sb[m][:].bitcast(F32)
+            for pair in range(2):
+                bank = transpose_four(x_in_words, 512 * pair, 256)
+                first = (4 * m + 2 * pair) * 256
+                regroup(pair == 0, x_grouped_words[:, first:first + 512], bank)
+        nc.vector.quantize_mx(
+            out=x_words[:].bitcast(FP8X4), scales=x_scales[:], in_=x_grouped[:]
+        )
 
         banks = {}
         grouped = {}
-        codes = {}
-        acc = {}
-        ytile = {}
+        packed = {}
+        sums = {}
+        y_tiles = {}
         stats = {}
 
-        def stage_t(k):
-            w32 = w_tiles[k][:].rearrange("p t k -> p (t k)").bitcast(F32)
-            for g in range(4):
-                banks[(k, g)] = transposes_into_bank(w32, 256 * g, 1024)
-            if k + W_AHEAD < NSLOT:
-                load_w(k + W_AHEAD)
+        def transpose_half(slot):
+            words = w_half[slot][:].rearrange("p t k -> p (t k)").bitcast(F32)
+            for g in range(PASSES):
+                banks[(slot, g)] = transpose_four(words, 256 * g, 1024)
+            if slot + W_AHEAD < SLOTS:
+                load_w(slot + W_AHEAD)
 
-        def stage_d(k, g):
-            blk = k // 2
-            tt = k % 2
+        def regroup_bank(slot, g):
+            block, tt = slot // 2, slot % 2
             if tt == 0:
-                grouped[(blk, g)] = gpool.tile([P, 2048], BF16, name="grp", align_bytes=64)
-            g32 = grouped[(blk, g)][:].bitcast(F32)
-            drain_bank(g == 3, g32[:, 512 * tt:512 * (tt + 1)], banks[(k, g)])
+                grouped[(block, g)] = gpool.tile([P, 2048], BF16, name="grp", align_bytes=64)
+            dst = grouped[(block, g)][:].bitcast(F32)
+            regroup(g == 3, dst[:, 512 * tt:512 * (tt + 1)], banks[(slot, g)])
 
-        def stage_q(blk, g):
-            cd = cpool.tile([P, 512], U32, name="cd", align_bytes=64)
-            sc = cpool.tile([P, 512], U8, name="sc", align_bytes=64)
+        def quantise(block, g):
+            words = cpool.tile([P, 512], U32, name="cd", align_bytes=64)
+            scales = cpool.tile([P, 512], U8, name="sc", align_bytes=64)
             nc.vector.quantize_mx(
-                out=cd[:].bitcast(FP8X4), scales=sc[:], in_=grouped[(blk, g)][:]
+                out=words[:].bitcast(FP8X4), scales=scales[:], in_=grouped[(block, g)][:]
             )
-            codes[(blk, g)] = (cd, sc)
+            packed[(block, g)] = (words, scales)
 
-        def stage_m(blk, gp):
+        def multiply(block, pair):
             for m in range(2):
-                if gp == 0:
-                    acc[(blk, m)] = opsum.tile([P, 512], F32, name="acc")
-                for g in (2 * gp, 2 * gp + 1):
-                    cd, sc = codes[(blk, g)]
-                    xcol = (4 * m + g) * P
+                if pair == 0:
+                    sums[(block, m)] = opsum.tile([P, 512], F32, name="acc")
+                for g in (2 * pair, 2 * pair + 1):
+                    words, scales = packed[(block, g)]
+                    c0 = (4 * m + g) * P
                     nc.tensor.matmul_mx(
-                        out=acc[(blk, m)][:],
-                        lhsT=xc[:, xcol:xcol + P].bitcast(FP8X4),
-                        lhsT_scale=xs[:, xcol:xcol + P],
-                        rhs=cd[:].bitcast(FP8X4),
-                        rhs_scale=sc[:],
+                        out=sums[(block, m)][:],
+                        lhsT=x_words[:, c0:c0 + P].bitcast(FP8X4),
+                        lhsT_scale=x_scales[:, c0:c0 + P],
+                        rhs=words[:].bitcast(FP8X4),
+                        rhs_scale=scales[:],
                         start=(g == 0),
-                        stop=(g == 3),
+                        stop=(g == PASSES - 1),
                     )
 
-        def qk_groups(i):
-            return [gq for gq in range(4) if (4 * i + gq) % 3 != 2]
+        def normed_groups(block):
+            return [n for n in range(4) if (4 * block + n) % 3 != 2]
 
-        def stage_a(i, m):
-            if i % 3 == 0:
-                ytile[(i // 3, m)] = ypool.tile([P, 1536], F32, name="y3")
-            off = 512 * (i % 3)
+        def add_bias(block, m):
+            if block % 3 == 0:
+                y_tiles[(block // 3, m)] = ypool.tile([P, 1536], F32, name="y3")
+            c0 = 512 * (block % 3)
             nc.vector.tensor_tensor(
-                out=ytile[(i // 3, m)][:, off:off + 512].rearrange("q (p t) -> q p t", t=4),
-                in0=acc[(i, m)][:].rearrange("q (t p) -> q p t", t=4),
-                in1=bias_bc[:, 512 * i:512 * (i + 1)].rearrange("q (p t) -> q p t", t=4),
+                out=y_tiles[(block // 3, m)][:, c0:c0 + 512].rearrange(
+                    "tok (p t) -> tok p t", t=4
+                ),
+                in0=sums[(block, m)][:].rearrange("tok (t p) -> tok p t", t=4),
+                in1=bias_all[:, 512 * block:512 * (block + 1)].rearrange(
+                    "tok (p t) -> tok p t", t=4
+                ),
                 op=ALU.add,
             )
 
-        def group_ap(i, m, gq):
-            off = 512 * (i % 3) + P * gq
-            return ytile[(i // 3, m)][:, off:off + P]
+        def group_of_y(block, m, n):
+            c0 = 512 * (block % 3) + HD * n
+            return y_tiles[(block // 3, m)][:, c0:c0 + HD]
 
-        def stage_sq(i, m, r):
-            groups = qk_groups(i)
-            n = len(groups)
-            if m == 0 and r == 0:
-                stats[(i, "ss")] = spool.tile([P, 2 * n], F32, name="ss")
-            sq = spool.tile([P, P], F32, name="sq")
-            col = m * n + r
+        def square_sum(block, m, i):
+            groups = normed_groups(block)
+            count = len(groups)
+            if m == 0 and i == 0:
+                stats[(block, "sum")] = spool.tile([P, 2 * count], F32, name="ss")
+            squares = spool.tile([P, HD], F32, name="sq")
+            col = m * count + i
             nc.scalar.activation(
-                out=sq[:],
-                in_=group_ap(i, m, groups[r]),
+                out=squares[:],
+                in_=group_of_y(block, m, groups[i]),
                 func=ACT.Square,
-                accum_out=stats[(i, "ss")][:, col:col + 1],
+                accum_out=stats[(block, "sum")][:, col:col + 1],
             )
 
-        def stage_max(i):
-            n = len(qk_groups(i))
-            stats[(i, "sc")] = spool.tile([P, 2 * n], F32, name="ssc")
+        def floor_sums(block):
+            count = len(normed_groups(block))
+            stats[(block, "floored")] = spool.tile([P, 2 * count], F32, name="ssc")
             nc.vector.tensor_scalar_max(
-                out=stats[(i, "sc")][:], in0=stats[(i, "ss")][:], scalar1=1e-24
+                out=stats[(block, "floored")][:], in0=stats[(block, "sum")][:], scalar1=1e-24
             )
 
-        def stage_sqrt(i):
-            n = len(qk_groups(i))
-            stats[(i, "nr")] = spool.tile([P, 2 * n], F32, name="nrm")
-            nc.scalar.sqrt(out=stats[(i, "nr")][:], in_=stats[(i, "sc")][:])
+        def root(block):
+            count = len(normed_groups(block))
+            stats[(block, "norm")] = spool.tile([P, 2 * count], F32, name="nrm")
+            nc.scalar.sqrt(out=stats[(block, "norm")][:], in_=stats[(block, "floored")][:])
 
-        def stage_recip(i):
-            n = len(qk_groups(i))
-            stats[(i, "rn")] = spool.tile([P, 2 * n], F32, name="rn")
-            nc.vector.reciprocal(out=stats[(i, "rn")][:], in_=stats[(i, "nr")][:])
+        def invert(block):
+            count = len(normed_groups(block))
+            stats[(block, "inverse")] = spool.tile([P, 2 * count], F32, name="rn")
+            nc.vector.reciprocal(out=stats[(block, "inverse")][:], in_=stats[(block, "norm")][:])
 
-        def stage_scale(i):
-            groups = qk_groups(i)
-            n = len(groups)
-            eng = nc.vector if i >= NBLK - 2 else nc.gpsimd
+        def scale(block):
+            groups = normed_groups(block)
+            count = len(groups)
+            engine = nc.vector if block >= BLOCKS - 2 else nc.gpsimd
             for m in range(2):
-                for r in range(n):
-                    ap = group_ap(i, m, groups[r])
-                    col = m * n + r
-                    eng.tensor_scalar(
-                        out=ap, in0=ap, scalar1=stats[(i, "rn")][:, col:col + 1],
+                for i in range(count):
+                    group = group_of_y(block, m, groups[i])
+                    col = m * count + i
+                    engine.tensor_scalar(
+                        out=group, in0=group,
+                        scalar1=stats[(block, "inverse")][:, col:col + 1],
                         scalar2=0.0, op0=ALU.mult, op1=ALU.add,
                     )
 
-        def flush(i, kinds):
-            if i % 3 != 2:
+        def store(block, kinds):
+            if block % 3 != 2:
                 return
-            sb = i // 3
-            for s in kinds:
+            four = block // 3
+            for kind in kinds:
                 for m in range(2):
                     for bl in range(2):
-                        view = ytile[(sb, m)][bl:P:2, :].rearrange(
-                            "q (h s c) -> q s h c", s=3, c=HD
+                        by_kind = y_tiles[(four, m)][bl:P:2, :].rearrange(
+                            "l (h kind c) -> l kind h c", kind=3, c=HD
                         )
                         nc.sync.dma_start(
-                            out=outs[s][2 * m + bl, 4 * sb:4 * sb + 4, :, :].rearrange(
+                            out=outs[kind][2 * m + bl, 4 * four:4 * four + 4, :, :].rearrange(
                                 "h l c -> l h c"
                             ),
-                            in_=view[:, s, :, :],
+                            in_=by_kind[:, kind, :, :],
                         )
 
-        def block_at(slot, lag):
-            v = slot - lag
-            if v >= 0 and v % 2 == 0 and v // 2 < NBLK:
-                return v // 2
+        def block_begun(slot, slots_ago):
+            first = slot - slots_ago
+            if first >= 0 and first % 2 == 0 and first // 2 < BLOCKS:
+                return first // 2
             return None
 
-        for k in range(NSLOT + 9):
-            i_rc = block_at(k, 8)
-            if i_rc is not None:
-                stage_recip(i_rc)
-                stage_scale(i_rc)
-                flush(i_rc, (0, 1))
-            i_mx = block_at(k, 7)
-            if i_mx is not None:
-                stage_max(i_mx)
-            i_a = block_at(k, 5)
-            if i_a is not None:
-                stage_a(i_a, 0)
-                stage_a(i_a, 1)
-                flush(i_a, (2,))
-            if k < NSLOT:
-                stage_t(k)
-            squares = []
-            if i_a is not None:
-                squares = [(i_a, 0, r) for r in range(len(qk_groups(i_a)))]
-            i_s1 = block_at(k, 6)
-            if i_s1 is not None:
-                squares = [(i_s1, 1, r) for r in range(len(qk_groups(i_s1)))]
-            if 0 <= k - 2 < NSLOT:
-                stage_q((k - 2) // 2, 2 * (k % 2))
-                stage_q((k - 2) // 2, 2 * (k % 2) + 1)
-            for j in range(4):
-                if k < NSLOT:
-                    stage_d(k, j)
-                if j < len(squares):
-                    stage_sq(*squares[j])
-            if i_mx is not None:
-                stage_sqrt(i_mx)
-            if 0 <= k - 3 < NSLOT:
-                stage_m((k - 3) // 2, (k - 3) % 2)
+        for slot in range(SLOTS + 9):
+            block = block_begun(slot, 8)
+            if block is not None:
+                invert(block)
+                scale(block)
+                store(block, (0, 1))
+            rooted = block_begun(slot, 7)
+            if rooted is not None:
+                floor_sums(rooted)
+            summed = block_begun(slot, 5)
+            if summed is not None:
+                add_bias(summed, 0)
+                add_bias(summed, 1)
+                store(summed, (2,))
+            if slot < SLOTS:
+                transpose_half(slot)
+            to_square = []
+            if summed is not None:
+                to_square = [(summed, 0, i) for i in range(len(normed_groups(summed)))]
+            second = block_begun(slot, 6)
+            if second is not None:
+                to_square = [(second, 1, i) for i in range(len(normed_groups(second)))]
+            if 0 <= slot - 2 < SLOTS:
+                quantise((slot - 2) // 2, 2 * (slot % 2))
+                quantise((slot - 2) // 2, 2 * (slot % 2) + 1)
+            for g in range(PASSES):
+                if slot < SLOTS:
+                    regroup_bank(slot, g)
+                if g < len(to_square):
+                    square_sum(*to_square[g])
+            if rooted is not None:
+                root(rooted)
+            if 0 <= slot - 3 < SLOTS:
+                multiply((slot - 3) // 2, (slot - 3) % 2)

from contextlib import ExitStack

import concourse.mybir as mybir
from concourse.masks import make_identity

F32 = mybir.dt.float32
BF16 = mybir.dt.bfloat16
U32 = mybir.dt.uint32
U8 = mybir.dt.uint8
I32 = mybir.dt.int32
FP8X4 = mybir.dt.float8_e4m3fn_x4
ALU = mybir.AluOpType
ACT = mybir.ActivationFunctionType

P = 128
E = 2048
HEADS = 16
HD = 128
PASSES = 4
BLOCKS = 12
SLOTS = 2 * BLOCKS
W_AHEAD = 12
T_BANKS = 6
FLOPS = 2 * 256 * 2048 * 6144


def tile_selfattention_pa_kernel(tc, x, W, b, out_0, out_1, out_2):
    nc = tc.nc
    outs = (out_0, out_1, out_2)
    with ExitStack() as ctx:
        const = ctx.enter_context(tc.tile_pool(name="const", bufs=1))
        wpool = ctx.enter_context(tc.tile_pool(name="wpool", bufs=W_AHEAD))
        gpool = ctx.enter_context(tc.tile_pool(name="gpool", bufs=8))
        cpool = ctx.enter_context(tc.tile_pool(name="cpool", bufs=6))
        ypool = ctx.enter_context(tc.tile_pool(name="ypool", bufs=6))
        spool = ctx.enter_context(tc.tile_pool(name="spool", bufs=4))
        tpsum = ctx.enter_context(tc.psum_pool(name="tpsum", bufs=T_BANKS))
        opsum = ctx.enter_context(tc.psum_pool(name="opsum", bufs=8 - T_BANKS))
        ctx.enter_context(tc.manual_schedule())

        ident_f = const.tile([P, P], F32, name="ident_f")
        ident_b = const.tile([P, P], BF16, name="ident_b")
        b_rows = const.tile([P, 384], BF16, name="b_sb")
        bias_all = const.tile([P, 6144], BF16, name="bias_bc")
        one = const.tile([P, 1], F32, name="warm")
        one_root = const.tile([P, 1], F32, name="warm2")
        x_sb = [const.tile([P, E], BF16, name="x_sb%d" % m) for m in range(2)]
        x_grouped = const.tile([P, 4096], BF16, name="xg", align_bytes=64)
        x_words = const.tile([P, 1024], U32, name="xc", align_bytes=64)
        x_scales = const.tile([P, 1024], U8, name="xs", align_bytes=64)

        w_half = {}

        def load_w(slot):
            block, tt = slot // 2, slot % 2
            rows = W[512 * block:512 * (block + 1), :].rearrange("(p t) k -> p t k", t=4)
            w_sb = wpool.tile([P, 2, E], BF16, name="w_sb")
            nc.sync.dma_start(out=w_sb[:], in_=rows[:, 2 * tt:2 * tt + 2, :])
            w_half[slot] = w_sb

        nc.vector.memset(b_rows[:].bitcast(I32), 0)
        nc.vector.memset(one[:], 1.0)
        nc.sync.dma_start(out=b_rows[0:16, :], in_=b.rearrange("(h n) -> h n", h=16))
        for m in range(2):
            for bl in range(2):
                nc.sync.dma_start(out=x_sb[m][bl:P:2, :], in_=x[2 * m + bl, :, :])
        for slot in range(W_AHEAD):
            load_w(slot)
        make_identity(nc, ident_b[:])
        make_identity(nc, ident_f[:])
        nc.scalar.sqrt(out=one_root[:], in_=one[:])

        def copy_out(on_vector, dst, src):
            if on_vector:
                nc.vector.tensor_copy(out=dst, in_=src)
            else:
                nc.scalar.copy(out=dst, in_=src)

        for h in range(HEADS):
            bank = tpsum.tile([P, 512], F32, name="tb")
            nc.tensor.matmul(
                out=bank[:, 0:384],
                lhsT=ident_b[:, h:h + 1].to_broadcast([P, P]),
                rhs=b_rows[:],
                start=True,
                stop=True,
            )
            copy_out(h % 2 == 0, bias_all[:, 384 * h:384 * (h + 1)], bank[:, 0:384])

        def transpose_four(words, first, step):
            bank = tpsum.tile([P, 512], F32, name="tb")
            for a in range(2):
                for u in range(2):
                    c0 = first + a * step + 128 * u
                    nc.tensor.transpose(
                        out=bank[:, (2 * a + u) * P:(2 * a + u + 1) * P],
                        in_=words[:, c0:c0 + P],
                        identity=ident_f[:],
                    )
            return bank

        def regroup(on_vector, dst_words, bank):
            copy_out(
                on_vector,
                dst_words.rearrange("p (a c u) -> p a c u", a=2, u=2),
                bank[:].rearrange("p (a u c) -> p a c u", a=2, u=2),
            )

        x_grouped_words = x_grouped[:].bitcast(F32)
        for m in range(2):
            x_in_words = x_sb[m][:].bitcast(F32)
            for pair in range(2):
                bank = transpose_four(x_in_words, 512 * pair, 256)
                first = (4 * m + 2 * pair) * 256
                regroup(pair == 0, x_grouped_words[:, first:first + 512], bank)
        nc.vector.quantize_mx(
            out=x_words[:].bitcast(FP8X4), scales=x_scales[:], in_=x_grouped[:]
        )

        banks = {}
        grouped = {}
        packed = {}
        sums = {}
        y_tiles = {}
        stats = {}

        def transpose_half(slot):
            words = w_half[slot][:].rearrange("p t k -> p (t k)").bitcast(F32)
            for g in range(PASSES):
                banks[(slot, g)] = transpose_four(words, 256 * g, 1024)
            if slot + W_AHEAD < SLOTS:
                load_w(slot + W_AHEAD)

        def regroup_bank(slot, g):
            block, tt = slot // 2, slot % 2
            if tt == 0:
                grouped[(block, g)] = gpool.tile([P, 2048], BF16, name="grp", align_bytes=64)
            dst = grouped[(block, g)][:].bitcast(F32)
            regroup(g == 3, dst[:, 512 * tt:512 * (tt + 1)], banks[(slot, g)])

        def quantise(block, g):
            words = cpool.tile([P, 512], U32, name="cd", align_bytes=64)
            scales = cpool.tile([P, 512], U8, name="sc", align_bytes=64)
            nc.vector.quantize_mx(
                out=words[:].bitcast(FP8X4), scales=scales[:], in_=grouped[(block, g)][:]
            )
            packed[(block, g)] = (words, scales)

        def multiply(block, pair):
            for m in range(2):
                if pair == 0:
                    sums[(block, m)] = opsum.tile([P, 512], F32, name="acc")
                for g in (2 * pair, 2 * pair + 1):
                    words, scales = packed[(block, g)]
                    c0 = (4 * m + g) * P
                    nc.tensor.matmul_mx(
                        out=sums[(block, m)][:],
                        lhsT=x_words[:, c0:c0 + P].bitcast(FP8X4),
                        lhsT_scale=x_scales[:, c0:c0 + P],
                        rhs=words[:].bitcast(FP8X4),
                        rhs_scale=scales[:],
                        start=(g == 0),
                        stop=(g == PASSES - 1),
                    )

        def normed_groups(block):
            return [n for n in range(4) if (4 * block + n) % 3 != 2]

        def add_bias(block, m):
            if block % 3 == 0:
                y_tiles[(block // 3, m)] = ypool.tile([P, 1536], F32, name="y3")
            c0 = 512 * (block % 3)
            nc.vector.tensor_tensor(
                out=y_tiles[(block // 3, m)][:, c0:c0 + 512].rearrange(
                    "tok (p t) -> tok p t", t=4
                ),
                in0=sums[(block, m)][:].rearrange("tok (t p) -> tok p t", t=4),
                in1=bias_all[:, 512 * block:512 * (block + 1)].rearrange(
                    "tok (p t) -> tok p t", t=4
                ),
                op=ALU.add,
            )

        def group_of_y(block, m, n):
            c0 = 512 * (block % 3) + HD * n
            return y_tiles[(block // 3, m)][:, c0:c0 + HD]

        def square_sum(block, m, i):
            groups = normed_groups(block)
            count = len(groups)
            if m == 0 and i == 0:
                stats[(block, "sum")] = spool.tile([P, 2 * count], F32, name="ss")
            squares = spool.tile([P, HD], F32, name="sq")
            col = m * count + i
            nc.scalar.activation(
                out=squares[:],
                in_=group_of_y(block, m, groups[i]),
                func=ACT.Square,
                accum_out=stats[(block, "sum")][:, col:col + 1],
            )

        def floor_sums(block):
            count = len(normed_groups(block))
            stats[(block, "floored")] = spool.tile([P, 2 * count], F32, name="ssc")
            nc.vector.tensor_scalar_max(
                out=stats[(block, "floored")][:], in0=stats[(block, "sum")][:], scalar1=1e-24
            )

        def root(block):
            count = len(normed_groups(block))
            stats[(block, "norm")] = spool.tile([P, 2 * count], F32, name="nrm")
            nc.scalar.sqrt(out=stats[(block, "norm")][:], in_=stats[(block, "floored")][:])

        def invert(block):
            count = len(normed_groups(block))
            stats[(block, "inverse")] = spool.tile([P, 2 * count], F32, name="rn")
            nc.vector.reciprocal(out=stats[(block, "inverse")][:], in_=stats[(block, "norm")][:])

        def scale(block):
            groups = normed_groups(block)
            count = len(groups)
            engine = nc.vector if block >= BLOCKS - 2 else nc.gpsimd
            for m in range(2):
                for i in range(count):
                    group = group_of_y(block, m, groups[i])
                    col = m * count + i
                    engine.tensor_scalar(
                        out=group, in0=group,
                        scalar1=stats[(block, "inverse")][:, col:col + 1],
                        scalar2=0.0, op0=ALU.mult, op1=ALU.add,
                    )

        def store(block, kinds):
            if block % 3 != 2:
                return
            four = block // 3
            for kind in kinds:
                for m in range(2):
                    for bl in range(2):
                        by_kind = y_tiles[(four, m)][bl:P:2, :].rearrange(
                            "l (h kind c) -> l kind h c", kind=3, c=HD
                        )
                        nc.sync.dma_start(
                            out=outs[kind][2 * m + bl, 4 * four:4 * four + 4, :, :].rearrange(
                                "h l c -> l h c"
                            ),
                            in_=by_kind[:, kind, :, :],
                        )

        def block_begun(slot, slots_ago):
            first = slot - slots_ago
            if first >= 0 and first % 2 == 0 and first // 2 < BLOCKS:
                return first // 2
            return None

        for slot in range(SLOTS + 9):
            block = block_begun(slot, 8)
            if block is not None:
                invert(block)
                scale(block)
                store(block, (0, 1))
            rooted = block_begun(slot, 7)
            if rooted is not None:
                floor_sums(rooted)
            summed = block_begun(slot, 5)
            if summed is not None:
                add_bias(summed, 0)
                add_bias(summed, 1)
                store(summed, (2,))
            if slot < SLOTS:
                transpose_half(slot)
            to_square = []
            if summed is not None:
                to_square = [(summed, 0, i) for i in range(len(normed_groups(summed)))]
            second = block_begun(slot, 6)
            if second is not None:
                to_square = [(second, 1, i) for i in range(len(normed_groups(second)))]
            if 0 <= slot - 2 < SLOTS:
                quantise((slot - 2) // 2, 2 * (slot % 2))
                quantise((slot - 2) // 2, 2 * (slot % 2) + 1)
            for g in range(PASSES):
                if slot < SLOTS:
                    regroup_bank(slot, g)
                if g < len(to_square):
                    square_sum(*to_square[g])
            if rooted is not None:
                root(rooted)
            if 0 <= slot - 3 < SLOTS:
                multiply((slot - 3) // 2, (slot - 3) % 2)
